import numpy as np
import ml_dtypes


def mxq(x, axis, fmt="e4m3"):
    dtype, down = {"e4m3": (ml_dtypes.float8_e4m3fn, 7), "e5m2": (ml_dtypes.float8_e5m2, 14)}[fmt]
    v = np.moveaxis(np.asarray(x, np.float32).astype(ml_dtypes.bfloat16).astype(np.float64), axis, -1)
    blocks = v.reshape(v.shape[:-1] + (-1, 32))
    amax = np.abs(blocks).max(-1, keepdims=True)
    byte = np.maximum(np.where(amax > 0, np.frexp(amax)[1] - 1 + 127, 0) - down, 1)
    scale = np.exp2(byte - 127.0)
    codes = (blocks / scale).astype(np.float32).astype(dtype).astype(np.float64)
    return np.moveaxis((codes * scale).reshape(v.shape), -1, axis)


WIDE = False


def mx_kscale(k):
    if not WIDE:
        return np.ones(k)
    levels = np.array([10, -10, 5, -5, 0])
    if k % 512:
        return np.exp2(np.random.permutation(np.resize(levels, k // 32))).repeat(32)
    a = np.empty((k // 512, 16))
    for p in range(k // 512):
        a[p, :8] = np.random.permutation(np.resize(levels, 8))
        for g in range(8):
            far = levels[np.abs(levels - a[p, g]) >= 10]
            a[p, g + 8] = far[np.random.randint(len(far))]
    return np.exp2(a.ravel()).repeat(32)


BF16 = ml_dtypes.bfloat16


def bf(x):
    return np.asarray(x, np.float32).astype(BF16)


def f64(x):
    return np.asarray(x).astype(np.float64)


B, N, E, F, H, K, C, G, DEG = 8, 2048, 512, 32, 64, 8, 32, 64, 32


def incidence(rows, cols):
    return (np.random.uniform(size=(rows, cols)) < DEG / N) * np.random.uniform(0.5, 1.5, (rows, cols))


def setup_inputs():
    s, t = mx_kscale(N), mx_kscale(E)
    return {"x": bf(np.random.standard_normal((B, N, C)) / s[None, :, None]),
            "rinc": bf(incidence(E, N) * s[None, :]),
            "linc": bf(incidence(N, E) * t[None, :]),
            "edge_w": bf(np.random.standard_normal((E, K)) * 0.25 / t[:, None])}


def reference(x, rinc, linc, edge_w):
    z = mxq(f64(rinc), 1, "e4m3") @ mxq(f64(x), 1, "e4m3")
    m = (z[:, :, :, None] * f64(edge_w)[None, :, None, :]).reshape(B, E, C * K)
    return mxq(f64(linc), 1, "e4m3") @ mxq(m, 1, "e4m3")

from contextlib import ExitStack

import concourse.mybir as mybir
from concourse.masks import make_identity

FP8X4 = mybir.dt.float8_e4m3fn_x4
BF16 = mybir.dt.bfloat16
F32 = mybir.dt.float32
U32 = mybir.dt.uint32
U8 = mybir.dt.uint8

P = 128
B, NODES, EDGES, C, KW = 8, 2048, 512, 32, 8
W = C * KW
J = NODES // P
FLOPS = 2 * EDGES * NODES * B * C + 2 * NODES * EDGES * B * W

STORES = ((1, 1, 2, 2, 2), (2, 2, 4), (4, 4), (4, 4), (4, 4), (4, 4), (4, 4), (4, 4))
ST_BUFS = {1: 2, 2: 5, 4: 8}

ORDER = (
    ("xr", 0), ("tr", 0, 0), ("xq", 0), ("cr", 0, 0, "S"), ("tr", 0, 1), ("cr", 0, 1, "V"),
    ("tr", 1, 0), ("rq", 0, 0), ("cr", 1, 0, "S"), ("tr", 1, 1), ("rq", 0, 1), ("tr", 2, 0),
    ("rq", 1, 0), ("cr", 1, 1, "S"), ("tr", 2, 1), ("rq", 1, 1), ("cr", 2, 0, "S"), ("cr", 2, 1, "V"),
    ("tr", 3, 0), ("tr", 3, 1), ("rq", 2, 0), ("cr", 3, 0, "S"), ("rq", 2, 1), ("cr", 3, 1, "S"),
    ("z", 0, 0, 0), ("rq", 3, 0), ("z", 0, 0, 1), ("z", 1, 0, 0), ("rq", 3, 1), ("z", 1, 0, 1),
    ("z", 2, 0, 0), ("z", 2, 0, 1), ("z", 3, 0, 0), ("z", 3, 0, 1), ("tl", 0, 0), ("m", 0),
    ("cl", 0, 0, "S"), ("tl", 0, 1), ("tl", 1, 0), ("tl", 1, 1), ("lq", 0, 0), ("cl", 0, 1, "S"),
    ("mq", 0), ("tl", 2, 0), ("cl", 1, 0, "S"), ("lq", 0, 1), ("tl", 2, 1), ("o", 0, 0),
    ("cl", 1, 1, "V"), ("cl", 2, 0, "S"), ("o", 0, 1), ("co", 0, 0, "V"), ("st", 0, 0), ("co", 0, 1, "S"),
    ("st", 0, 1), ("tl", 3, 0), ("lq", 1, 0), ("tl", 3, 1), ("cl", 2, 1, "S"), ("lq", 1, 1),
    ("lq", 2, 0), ("o", 0, 2), ("cl", 3, 0, "S"), ("lq", 2, 1), ("o", 0, 3), ("co", 0, 2, "S"),
    ("m", 1), ("o", 0, 4), ("o", 0, 5), ("co", 0, 3, "S"), ("st", 0, 2), ("lq", 3, 0),
    ("cl", 3, 1, "S"), ("co", 0, 4, "V"), ("co", 0, 5, "S"), ("st", 0, 4), ("o", 0, 6), ("lq", 3, 1),
    ("mq", 1), ("co", 0, 6, "S"), ("o", 0, 7), ("m", 2), ("co", 0, 7, "S"), ("st", 0, 6),
    ("o", 1, 0), ("o", 1, 1), ("co", 1, 0, "S"), ("o", 1, 2), ("co", 1, 1, "V"), ("st", 1, 0),
    ("o", 1, 3), ("co", 1, 2, "S"), ("o", 1, 4), ("co", 1, 3, "V"), ("st", 1, 2), ("o", 1, 5),
    ("o", 1, 6), ("co", 1, 4, "S"), ("mq", 2), ("o", 1, 7), ("co", 1, 5, "V"), ("co", 1, 6, "S"),
    ("o", 2, 0), ("co", 1, 7, "S"), ("st", 1, 4), ("co", 2, 0, "V"), ("o", 2, 1), ("o", 2, 2),
    ("co", 2, 1, "S"), ("o", 2, 3), ("co", 2, 2, "V"), ("o", 2, 4), ("co", 2, 3, "S"), ("st", 2, 0),
    ("o", 2, 5), ("m", 3), ("o", 2, 6), ("co", 2, 4, "S"), ("o", 2, 7), ("co", 2, 5, "S"),
    ("mq", 3), ("co", 2, 6, "S"), ("co", 2, 7, "V"), ("st", 2, 4), ("o", 3, 0), ("co", 3, 0, "S"),
    ("xr", 1), ("o", 3, 1), ("o", 3, 2), ("co", 3, 1, "S"), ("o", 3, 3), ("o", 3, 4),
    ("o", 3, 5), ("xq", 1), ("co", 3, 2, "S"), ("o", 3, 6), ("o", 3, 7), ("co", 3, 3, "S"),
    ("st", 3, 0), ("co", 3, 4, "V"), ("z", 0, 1, 0), ("co", 3, 5, "S"), ("z", 0, 1, 1), ("co", 3, 6, "V"),
    ("z", 1, 1, 0), ("z", 1, 1, 1), ("co", 3, 7, "S"), ("st", 3, 4), ("z", 2, 1, 0), ("z", 2, 1, 1),
    ("z", 3, 1, 0), ("z", 3, 1, 1), ("m", 4), ("mq", 4), ("m", 5), ("o", 4, 0),
    ("co", 4, 0, "S"), ("o", 4, 1), ("o", 4, 2), ("co", 4, 1, "V"), ("co", 4, 2, "S"), ("o", 4, 3),
    ("o", 4, 4), ("co", 4, 3, "V"), ("st", 4, 0), ("o", 4, 5), ("co", 4, 4, "S"), ("o", 4, 6),
    ("mq", 5), ("o", 4, 7), ("co", 4, 5, "S"), ("co", 4, 6, "V"), ("co", 4, 7, "S"), ("st", 4, 4),
    ("o", 5, 0), ("co", 5, 0, "V"), ("o", 5, 1), ("co", 5, 1, "S"), ("o", 5, 2), ("o", 5, 3),
    ("co", 5, 2, "V"), ("co", 5, 3, "S"), ("st", 5, 0), ("o", 5, 4), ("o", 5, 5), ("m", 6),
    ("o", 5, 6), ("co", 5, 4, "S"), ("o", 5, 7), ("co", 5, 5, "S"), ("mq", 6), ("co", 5, 6, "S"),
    ("co", 5, 7, "V"), ("st", 5, 4), ("o", 6, 0), ("co", 6, 0, "S"), ("o", 6, 1), ("m", 7),
    ("o", 6, 2), ("co", 6, 1, "S"), ("o", 6, 3), ("o", 6, 4), ("co", 6, 2, "V"), ("o", 6, 5),
    ("co", 6, 3, "S"), ("st", 6, 0), ("o", 6, 6), ("mq", 7), ("o", 6, 7), ("co", 6, 4, "S"),
    ("co", 6, 5, "V"), ("co", 6, 6, "S"), ("o", 7, 0), ("co", 6, 7, "V"), ("st", 6, 4), ("o", 7, 1),
    ("co", 7, 0, "S"), ("o", 7, 2), ("co", 7, 1, "V"), ("o", 7, 3), ("co", 7, 2, "S"), ("o", 7, 4),
    ("co", 7, 3, "V"), ("st", 7, 0), ("o", 7, 5), ("co", 7, 4, "S"), ("o", 7, 6), ("o", 7, 7),
    ("co", 7, 5, "V"), ("co", 7, 6, "S"), ("co", 7, 7, "V"), ("st", 7, 4),
)


def tile_sgcn_pa_t_kernel(tc, x, rinc, linc, edge_w, out):
    nc = tc.nc
    with ExitStack() as ctx:
        keep = ctx.enter_context(tc.tile_pool(name="keep", bufs=1))
        stage = ctx.enter_context(tc.tile_pool(name="stage", bufs=1))
        ps_z = ctx.enter_context(tc.psum_pool(name="ps_z", bufs=1))
        ps = ctx.enter_context(tc.psum_pool(name="ps", bufs=6))
        ctx.enter_context(tc.manual_schedule())

        ident = keep.tile([P, P], F32, name="ident")
        make_identity(nc, ident[:])

        ew_raw = keep.tile([P, 4 * KW], BF16, name="ew_raw")
        nc.scalar.dma_start(out=ew_raw[:], in_=edge_w.rearrange("(p t) k -> p (t k)", t=4))

        xs = [keep.tile([P, 4, 4, 4 * C], BF16, name="xs%d" % h) for h in range(2)]
        rs_whole = [keep.tile([P, NODES], BF16, name="rs%d" % te) for te in range(3)]
        rs_last = [keep.tile([P, NODES // 2], BF16, name="rs3_%d" % k) for k in range(2)]
        ls = [keep.tile([P, 4, EDGES], BF16, name="ls%d" % q) for q in range(4)]
        r_view = rinc.rearrange("(p t) n -> t p n", t=4)
        l_view = linc.rearrange("(p j) e -> p j e", j=J)

        def load_x(h):
            nc.sync.dma_start(out=xs[h][:], in_=x[4 * h:4 * h + 4].rearrange("b (g p t) c -> p b g (t c)", g=4, p=P, t=4))

        load_x(0)
        for te in range(3):
            nc.sync.dma_start(out=rs_whole[te][:], in_=r_view[te])
        for k in range(2):
            nc.sync.dma_start(out=rs_last[k][:], in_=r_view[3][:, 1024 * k:1024 * (k + 1)])
        for q in range(4):
            nc.sync.dma_start(out=ls[q][:], in_=l_view[:, 4 * q:4 * q + 4, :])
        load_x(1)

        ewf = keep.tile([P, KW, 4], F32, name="ewf")
        nc.vector.tensor_copy(
            out=ewf[:],
            in_=ew_raw[:].rearrange("p (t k) -> p k t", t=4),
        )

        z = [ps_z.tile([P, 4, P], F32, name="z%d" % h) for h in range(2)]
        o_view = out.rearrange("b (p j) w -> b p j w", j=J)
        live = {}

        def copy(eng, dst, src):
            if eng == "V":
                nc.vector.tensor_copy(out=dst, in_=src)
            else:
                nc.scalar.copy(out=dst, in_=src)

        def quant(key, width, src):
            cd = keep.tile([P, width // 4], U32, name="c_%s_%d_%d" % key, align_bytes=64)
            sc = keep.tile([P, width // 4], U8, name="s_%s_%d_%d" % key, align_bytes=64)
            nc.vector.quantize_mx(out=cd[:].bitcast(FP8X4), scales=sc[:], in_=src)
            live[key] = (cd, sc)

        def op_xr(h):
            xg = keep.tile([P, 4, P * 4], BF16, name="xg%d" % h, align_bytes=64)
            for g in range(4):
                nc.vector.tensor_copy(
                    out=xg[:, g, :].rearrange("p (b c t) -> p b c t", b=4, c=C),
                    in_=xs[h][:, :, g, :].rearrange("p b (t c) -> p b c t", t=4),
                )
            live[("xg", h)] = xg

        def op_xq(h):
            quant(("x", h, 0), 2048, live[("xg", h)][:].rearrange("p g w -> p (g w)"))

        def op_tr(te, k):
            tp = ps.tile([P, 2, 2, P], F32, name="tp", tag="bank")
            rw = (rs_whole[te][:, 1024 * k:1024 * (k + 1)] if te < 3 else rs_last[k][:]).bitcast(F32)
            for gg in range(2):
                for h in range(2):
                    nc.tensor.transpose(tp[:, gg, h, :], rw[:, 256 * gg + h:256 * (gg + 1):2], ident[:])
            live[("tr", te, k)] = tp

        def op_cr(te, k, eng):
            rg = keep.tile([P, 2 * P * 4], BF16, name="rg%d_%d" % (te, k), align_bytes=64)
            copy(eng, rg[:].bitcast(F32).rearrange("p (g e h) -> p g e h", g=2, h=2),
                 live[("tr", te, k)][:].rearrange("p g h e -> p g e h"))
            live[("rg", te, k)] = rg

        def op_rq(te, k):
            quant(("r", te, k), 1024, live[("rg", te, k)][:])

        def op_z(te, h, k):
            cd, sc = live[("r", te, k)]
            xc, xsc = live[("x", h, 0)]
            for gg in range(2):
                g = 2 * k + gg
                nc.tensor.matmul_mx(
                    out=z[h][:, te, :],
                    lhsT=cd[:, P * gg:P * (gg + 1)].bitcast(FP8X4),
                    lhsT_scale=sc[:, P * gg:P * (gg + 1)],
                    rhs=xc[:, P * g:P * (g + 1)].bitcast(FP8X4),
                    rhs_scale=xsc[:, P * g:P * (g + 1)],
                    start=(g == 0),
                    stop=(g == 3),
                )

        def op_tl(q, k):
            tp = ps.tile([P, 2, 2, P], F32, name="tp", tag="bank")
            lw = ls[q][:].bitcast(F32)
            for jj in range(2):
                for u in range(2):
                    nc.tensor.transpose(tp[:, jj, u, :], lw[:, 2 * k + jj, u:2 * P:2], ident[:])
            live[("tl", q, k)] = tp

        def op_cl(q, k, eng):
            lg = keep.tile([P, 2 * P * 4], BF16, name="lg%d_%d" % (q, k), align_bytes=64)
            copy(eng, lg[:].bitcast(F32).rearrange("p (j n u) -> p j n u", j=2, u=2),
                 live[("tl", q, k)][:].rearrange("p j u n -> p j n u"))
            live[("lg", q, k)] = lg

        def op_lq(q, k):
            quant(("l", q, k), 1024, live[("lg", q, k)][:])

        def op_m(b):
            mg = keep.tile([P, W * 4], BF16, name="mg%d" % b, align_bytes=64)
            nc.vector.tensor_tensor(
                out=mg[:].rearrange("p (c k t) -> p c k t", c=C, k=KW),
                in0=z[b // 4][:, :, C * (b % 4):C * (b % 4 + 1)].rearrange("p t c -> p c t").unsqueeze(2).to_broadcast([P, C, KW, 4]),
                in1=ewf[:].unsqueeze(1).to_broadcast([P, C, KW, 4]),
                op=mybir.AluOpType.mult,
            )
            live[("mg", b)] = mg

        def op_mq(b):
            quant(("m", b, 0), 1024, live[("mg", b)][:])

        def op_o(b, jp):
            o = ps.tile([P, 2, W], F32, name="o", tag="bank")
            cd, sc = live[("l", jp // 2, jp % 2)]
            mc, ms = live[("m", b, 0)]
            for jj in range(2):
                nc.tensor.matmul_mx(
                    out=o[:, jj, :],
                    lhsT=cd[:, P * jj:P * (jj + 1)].bitcast(FP8X4),
                    lhsT_scale=sc[:, P * jj:P * (jj + 1)],
                    rhs=mc[:].bitcast(FP8X4),
                    rhs_scale=ms[:],
                    start=True,
                    stop=True,
                )
            live[("o", b, jp)] = o

        def group_of(b, jp):
            j0 = 0
            for n in STORES[b]:
                if jp < j0 + n:
                    return j0, n
                j0 += n
            return None

        def op_co(b, jp, eng):
            j0, n = group_of(b, jp)
            if ("st", b, j0) not in live:
                live[("st", b, j0)] = stage.tile([P, 2 * n, W], F32, name="st%d" % n, bufs=ST_BUFS[n])
            st = live[("st", b, j0)]
            copy(eng, st[:, 2 * (jp - j0):2 * (jp - j0) + 2, :], live[("o", b, jp)][:])

        def op_st(b, j0):
            n = group_of(b, j0)[1]
            nc.sync.dma_start(out=o_view[b, :, 2 * j0:2 * (j0 + n), :], in_=live[("st", b, j0)][:])

        table = {"xr": op_xr, "xq": op_xq, "tr": op_tr, "cr": op_cr, "rq": op_rq, "z": op_z, "tl": op_tl,
                 "cl": op_cl, "lq": op_lq, "m": op_m, "mq": op_mq, "o": op_o, "co": op_co, "st": op_st}
        for step in ORDER:
            table[step[0]](*step[1:])
